import numpy as np
import ml_dtypes


def mxq(x, axis, fmt="e4m3"):
    dtype, down = {"e4m3": (ml_dtypes.float8_e4m3fn, 7), "e5m2": (ml_dtypes.float8_e5m2, 14)}[fmt]
    v = np.moveaxis(np.asarray(x, np.float32).astype(ml_dtypes.bfloat16).astype(np.float64), axis, -1)
    blocks = v.reshape(v.shape[:-1] + (-1, 32))
    amax = np.abs(blocks).max(-1, keepdims=True)
    byte = np.maximum(np.where(amax > 0, np.frexp(amax)[1] - 1 + 127, 0) - down, 1)
    scale = np.exp2(byte - 127.0)
    codes = (blocks / scale).astype(np.float32).astype(dtype).astype(np.float64)
    return np.moveaxis((codes * scale).reshape(v.shape), -1, axis)


WIDE = False


def mx_kscale(k):
    if not WIDE:
        return np.ones(k)
    levels = np.array([10, -10, 5, -5, 0])
    a = np.random.permutation(np.resize(levels, k // 512 * 4)).reshape(k // 512, 4)
    idx = np.arange(k)
    return np.exp2(a[idx // 512, idx % 128 // 32])


BF16 = ml_dtypes.bfloat16


def bf(x):
    return np.asarray(x, np.float32).astype(BF16)


def f64(x):
    return np.asarray(x).astype(np.float64)


B, S, D, NH, HD, HID = 4, 256, 768, 4, 256, 1024


def setup_inputs():
    t = mx_kscale(HID)
    lengths = np.random.randint(S // 2, S + 1, size=B)
    tail = 0.05 + 0.45 * np.random.random_sample((B, S))
    mask = np.where(np.arange(S)[None, :] < lengths[:, None], 1.0, tail)
    h = np.random.standard_normal((NH, B, S, HD)) + 0.3 * np.random.standard_normal((NH, 1, 1, HD))
    return {"h_heads": bf(h),
            "attention_mask": bf(mask),
            "W1": bf(np.random.standard_normal((NH, HID, HD)) / np.sqrt(HD) * t[None, :, None]),
            "b1": bf(np.random.standard_normal((NH, HID)) * 0.2 * t[None, :]),
            "W2": bf(np.random.standard_normal((NH, HD, HID)) * 2.5 / np.sqrt(HID) / t[None, None, :])}


def reference(h_heads, attention_mask, W1, b1, W2):
    h = f64(h_heads)
    pre = h.reshape(NH, B * S, HD) @ f64(W1).transpose(0, 2, 1) + f64(b1)[:, None, :]
    hid = np.maximum(pre, 0.0)
    a = mxq(hid, 2, "e4m3") @ mxq(f64(W2), 2, "e4m3").transpose(0, 2, 1)
    with np.errstate(divide="ignore"):
        log_mask = np.log(f64(attention_mask))[None, :, :, None]
    a = a.reshape(NH, B, S, HD) + log_mask
    e = np.exp(a - a.max(axis=2, keepdims=True))
    w = e / e.sum(axis=2, keepdims=True)
    v = (h * w).sum(axis=2)
    return v.transpose(1, 0, 2).reshape(B, NH * HD)

@@ -1,0 +1,235 @@
+from contextlib import ExitStack
+
+import concourse.mybir as mybir
+from concourse.masks import make_identity
+
+FLOPS = 2 * 2 * 4 * 1024 * 1024 * 256
+
+F32 = mybir.dt.float32
+BF16 = mybir.dt.bfloat16
+U32 = mybir.dt.uint32
+U8 = mybir.dt.uint8
+FP8X4 = mybir.dt.float8_e4m3fn_x4
+ACT = mybir.ActivationFunctionType
+ALU = mybir.AluOpType
+AX = mybir.AxisListType
+
+P = 128
+NH = 4
+
+
+def tile_multiheadgeneralizedpooling_pa_kernel(tc, h_heads, attention_mask, W1, b1, W2, out):
+    nc = tc.nc
+    with ExitStack() as ctx:
+        keep = ctx.enter_context(tc.tile_pool(name="keep", bufs=1))
+        work = ctx.enter_context(tc.tile_pool(name="work", bufs=3))
+        psum = ctx.enter_context(tc.psum_pool(name="psum", bufs=2))
+
+        h_raw = []
+        w1_raw = []
+        w2_raw = []
+        for i in range(NH):
+            h_raw.append(keep.tile([P, 2048], BF16, name="h_raw%d" % i))
+            w1_raw.append(keep.tile([P, 2048], BF16, name="w1_raw%d" % i))
+            w2_raw.append(keep.tile([P, 2048], BF16, name="w2_raw%d" % i))
+        b1_raw = keep.tile([P, 256], BF16, name="b1_raw")
+        mask_raw = keep.tile([P, 1024], BF16, name="mask_raw")
+        res = keep.tile([P, 2, P], F32, name="res")
+        ident = keep.tile([P, P], F32, name="ident")
+
+        nc.vector.memset(b1_raw[:], 0.0)
+        nc.vector.memset(res[:], 0.0)
+        make_identity(nc, ident[:])
+
+        for i in range(NH):
+            hsrc = h_heads[i].rearrange("b (p n) f -> p b (n f)", n=2)
+            hdst = h_raw[i][:].rearrange("p (b x) -> p b x", b=4)
+            wsrc = W1[i].rearrange("(x p e) f -> p x (e f)", x=4, e=2)
+            wdst = w1_raw[i][:].rearrange("p (x y) -> p x y", x=4)
+            if i == 0:
+                nc.sync.dma_start(out=hdst[:, 0:2, :], in_=hsrc[:, 0:2, :])
+                nc.sync.dma_start(out=wdst[:, 0:2, :], in_=wsrc[:, 0:2, :])
+                nc.sync.dma_start(out=wdst[:, 2:4, :], in_=wsrc[:, 2:4, :])
+                nc.sync.dma_start(out=hdst[:, 2:4, :], in_=hsrc[:, 2:4, :])
+            else:
+                nc.sync.dma_start(out=hdst, in_=hsrc)
+                nc.sync.dma_start(out=wdst, in_=wsrc)
+            nc.sync.dma_start(out=w2_raw[i][:], in_=W2[i].rearrange("(p e) k -> p (e k)", e=2))
+        nc.scalar.dma_start(out=b1_raw[0:16, :], in_=b1.rearrange("i (r k) -> (i r) k", k=256))
+        nc.gpsimd.dma_start(
+            out=mask_raw[:], in_=attention_mask.rearrange("b s -> (b s)").partition_broadcast(P)
+        )
+
+        tpb = psum.tile([P, 4, P], F32, tag="tp", name="tpb")
+        nc.tensor.transpose(out=tpb[:, 0, :], in_=b1_raw[:].bitcast(F32), identity=ident[:])
+        bias_w = keep.tile([P, 16], F32, name="bias_w")
+        nc.vector.tensor_copy(out=bias_w[:], in_=tpb[:, 0, 0:16])
+        bias = keep.tile([P, 32], F32, name="bias")
+        nc.vector.tensor_copy(out=bias[:], in_=bias_w[:].bitcast(BF16))
+
+        nlnm = keep.tile([P, 1024], F32, name="nlnm")
+        nc.scalar.activation(
+            out=nlnm[:].rearrange("q (b n p) -> q b n p", b=4, n=2),
+            in_=mask_raw[:].rearrange("q (b p n) -> q b n p", b=4, n=2),
+            func=ACT.Ln,
+        )
+        nc.vector.tensor_scalar_mul(out=nlnm[:], in0=nlnm[:], scalar1=-1.0)
+
+        num = keep.tile([P, 32], F32, name="num")
+        den = keep.tile([P, 32], F32, name="den")
+
+        hT_b = [None] * NH
+        w1T_b = [None] * NH
+        w2c = [None] * NH
+        w2s = [None] * NH
+
+        def prep(i):
+            hw = h_raw[i][:].bitcast(F32)
+            ww = w1_raw[i][:].bitcast(F32)
+            vw = w2_raw[i][:].bitcast(F32)
+            hT = keep.tile([P, 1024], F32, name="hT%d" % i)
+            w1T = keep.tile([P, 1024], F32, name="w1T%d" % i)
+            w2g = keep.tile([P, 1024], F32, name="w2g%d" % i, align_bytes=64)
+            for half in range(2):
+                tp = psum.tile([P, 4, P], F32, tag="tp", name="tph")
+                for k in range(4):
+                    blk = half * 4 + k
+                    nc.tensor.transpose(out=tp[:, k, :], in_=hw[:, blk * P:(blk + 1) * P], identity=ident[:])
+                nc.vector.tensor_copy(
+                    out=hT[:, half * 512:(half + 1) * 512], in_=tp[:].rearrange("q k p -> q (k p)")
+                )
+                tp = psum.tile([P, 4, P], F32, tag="tp", name="tpw")
+                for k in range(4):
+                    blk = half * 4 + k
+                    nc.tensor.transpose(out=tp[:, k, :], in_=ww[:, blk * P:(blk + 1) * P], identity=ident[:])
+                nc.scalar.copy(
+                    out=w1T[:, half * 512:(half + 1) * 512], in_=tp[:].rearrange("q k p -> q (k p)")
+                )
+            for g in range(2):
+                tp = psum.tile([P, 4, P], F32, tag="tp", name="tpv")
+                for e in range(2):
+                    for u in range(2):
+                        off = e * 512 + (g * 2 + u) * P
+                        nc.tensor.transpose(out=tp[:, e * 2 + u, :], in_=vw[:, off:off + P], identity=ident[:])
+                nc.scalar.copy(
+                    out=w2g[:, g * 512:(g + 1) * 512].rearrange("q (e p u) -> q e p u", e=2, u=2),
+                    in_=tp[:].rearrange("q (e u) p -> q e p u", e=2),
+                )
+            codes = keep.tile([P, 512], U32, name="w2c%d" % i, align_bytes=64)
+            scales = keep.tile([P, 512], U8, name="w2s%d" % i, align_bytes=64)
+            nc.vector.quantize_mx(out=codes[:].bitcast(FP8X4), scales=scales[:], in_=w2g[:].bitcast(BF16))
+            hT_b[i] = hT[:].bitcast(BF16).rearrange("q (m e) -> q m e", e=2)
+            w1T_b[i] = w1T[:].bitcast(BF16).rearrange("q (m e) -> q m e", e=2)
+            w2c[i] = codes
+            w2s[i] = scales
+
+        def first_matmul(i, c, g, hc, hs):
+            hidp = work.tile([P, 4, 512], BF16, tag="hidp", name="hidp")
+            for t in range(4):
+                blk = g * 4 + t
+                pre = psum.tile([P, 512], F32, tag="pre", name="pre", bufs=4)
+                for e in range(2):
+                    nc.tensor.matmul(
+                        out=pre[:],
+                        lhsT=w1T_b[i][:, blk * P:(blk + 1) * P, e],
+                        rhs=hT_b[i][:, c * 512:(c + 1) * 512, e],
+                        start=(e == 0),
+                        stop=(e == 1),
+                    )
+                col = i * 8 + blk
+                nc.scalar.activation(
+                    out=hidp[:, t, :], in_=pre[:], func=ACT.Relu, bias=bias[:, col:col + 1], scale=1.0
+                )
+            grouped = work.tile([P, 512, 4], BF16, tag="grouped", name="grouped", align_bytes=64)
+            nc.vector.tensor_copy(
+                out=grouped[:].rearrange("p (a r) t -> p a t r", r=4),
+                in_=hidp[:].rearrange("p t (a r) -> p a t r", r=4),
+            )
+            nc.vector.quantize_mx(
+                out=hc[:, g, :].bitcast(FP8X4),
+                scales=hs[:, g, :],
+                in_=grouped[:].rearrange("p w t -> p (w t)"),
+            )
+
+        def second_matmul(i, hc, hs):
+            att = []
+            for e in range(2):
+                a = psum.tile([P, 512], F32, tag="att", name="att")
+                for g in range(2):
+                    lo = (g * 2 + e) * P
+                    nc.tensor.matmul_mx(
+                        out=a[:],
+                        lhsT=w2c[i][:, lo:lo + P].bitcast(FP8X4),
+                        lhsT_scale=w2s[i][:, lo:lo + P],
+                        rhs=hc[:, g, :].bitcast(FP8X4),
+                        rhs_scale=hs[:, g, :],
+                        start=(g == 0),
+                        stop=(g == 1),
+                    )
+                att.append(a)
+            return att
+
+        def softmax(i, c, att):
+            tneg = work.tile([P, 2, 512], F32, tag="tneg", name="tneg")
+            for e in range(2):
+                nc.vector.tensor_tensor(
+                    out=tneg[:, e, :], in0=nlnm[:, c * 512:(c + 1) * 512], in1=att[e][:], op=ALU.subtract
+                )
+            minv = work.tile([P, 4], F32, tag="minv", name="minv")
+            nc.vector.tensor_reduce(
+                out=minv[:], in_=tneg[:].rearrange("p e (s w) -> p (e s) w", w=256), axis=AX.X, op=ALU.min
+            )
+            for e in range(2):
+                for s in range(2):
+                    col = e * 16 + (2 * c + s) * 4 + i
+                    ex = work.tile([P, 256], F32, tag="ex", name="ex", bufs=4)
+                    nc.scalar.activation(
+                        out=ex[:],
+                        in_=tneg[:, e, s * 256:(s + 1) * 256],
+                        func=ACT.Exp,
+                        bias=minv[:, e * 2 + s:e * 2 + s + 1],
+                        scale=-1.0,
+                        accum_out=den[:, col:col + 1],
+                    )
+                    junk = work.tile([P, 256], F32, tag="junk", name="junk", bufs=2)
+                    lo = c * 512 + s * 256
+                    nc.vector.scalar_tensor_tensor(
+                        out=junk[:],
+                        in0=ex[:],
+                        scalar=1.0,
+                        in1=hT_b[i][:, lo:lo + 256, e],
+                        op0=ALU.mult,
+                        op1=ALU.mult,
+                        accum_out=num[:, col:col + 1],
+                    )
+
+        prep(0)
+        for j in range(2 * NH):
+            i = j // 2
+            c = j % 2
+            hc = work.tile([P, 2, 512], U32, tag="hc", name="hc", align_bytes=64)
+            hs = work.tile([P, 2, 512], U8, tag="hs", name="hs", align_bytes=64)
+            first_matmul(i, c, 0, hc, hs)
+            first_matmul(i, c, 1, hc, hs)
+            if c == 0 and i + 1 < NH:
+                prep(i + 1)
+            att = second_matmul(i, hc, hs)
+            softmax(i, c, att)
+
+        rden = keep.tile([P, 32], F32, name="rden")
+        nc.vector.reciprocal(out=rden[:], in_=den[:])
+        nc.vector.tensor_tensor(
+            out=res[:, :, 0:16],
+            in0=num[:].rearrange("p (e x) -> p e x", e=2),
+            in1=rden[:].rearrange("p (e x) -> p e x", e=2),
+            op=ALU.mult,
+        )
+        tpo = psum.tile([P, 4, P], F32, tag="tp", name="tpo")
+        for e in range(2):
+            nc.tensor.transpose(out=tpo[:, e, :], in_=res[:, e, :], identity=ident[:])
+        o_sb = keep.tile([P, 256], F32, name="o_sb")
+        nc.scalar.copy(
+            out=o_sb[0:16, :].rearrange("r (p e) -> r p e", e=2),
+            in_=tpo[0:16, 0:2, :].rearrange("r e p -> r p e"),
+        )
+        nc.sync.dma_start(out=out.rearrange("b (i f) -> (b i) f", i=4), in_=o_sb[0:16, :])

@@ -16,6 +16,8 @@ AX = mybir.AxisListType
 
 P = 128
 NH = 4
+CHUNKS = 2 * NH
+HALVES = 2 * CHUNKS
 
 
 def tile_multiheadgeneralizedpooling_pa_kernel(tc, h_heads, attention_mask, W1, b1, W2, out):
@@ -24,28 +26,38 @@ def tile_multiheadgeneralizedpooling_pa_kernel(tc, h_heads, attention_mask, W1, 
         keep = ctx.enter_context(tc.tile_pool(name="keep", bufs=1))
         work = ctx.enter_context(tc.tile_pool(name="work", bufs=3))
         psum = ctx.enter_context(tc.psum_pool(name="psum", bufs=2))
+        ctx.enter_context(tc.manual_schedule())
 
-        h_raw = []
-        w1_raw = []
-        w2_raw = []
+        raw = {}
+        turned = {}
         for i in range(NH):
-            h_raw.append(keep.tile([P, 2048], BF16, name="h_raw%d" % i))
-            w1_raw.append(keep.tile([P, 2048], BF16, name="w1_raw%d" % i))
-            w2_raw.append(keep.tile([P, 2048], BF16, name="w2_raw%d" % i))
+            for kind in ("h", "w1", "w2"):
+                raw[(kind, i)] = keep.tile([P, 2048], BF16, name="raw_%s%d" % (kind, i))
+                turned[(kind, i)] = keep.tile([P, 1024], F32, name="turned_%s%d" % (kind, i), align_bytes=64)
+        w2c = [keep.tile([P, 512], U32, name="w2c%d" % i, align_bytes=64) for i in range(NH)]
+        w2s = [keep.tile([P, 512], U8, name="w2s%d" % i, align_bytes=64) for i in range(NH)]
+        hT_b = [turned[("h", i)][:].bitcast(BF16).rearrange("q (m e) -> q m e", e=2) for i in range(NH)]
+        w1T_b = [turned[("w1", i)][:].bitcast(BF16).rearrange("q (m e) -> q m e", e=2) for i in range(NH)]
         b1_raw = keep.tile([P, 256], BF16, name="b1_raw")
         mask_raw = keep.tile([P, 1024], BF16, name="mask_raw")
         res = keep.tile([P, 2, P], F32, name="res")
         ident = keep.tile([P, P], F32, name="ident")
+        bias_w = keep.tile([P, 16], F32, name="bias_w")
+        bias = keep.tile([P, 32], F32, name="bias")
+        nlnm = keep.tile([P, 1024], F32, name="nlnm")
+        num = keep.tile([P, 32], F32, name="num")
+        den = keep.tile([P, 32], F32, name="den")
 
         nc.vector.memset(b1_raw[:], 0.0)
         nc.vector.memset(res[:], 0.0)
         make_identity(nc, ident[:])
 
+        nc.scalar.dma_start(out=b1_raw[0:16, :], in_=b1.rearrange("i (r k) -> (i r) k", k=256))
         for i in range(NH):
             hsrc = h_heads[i].rearrange("b (p n) f -> p b (n f)", n=2)
-            hdst = h_raw[i][:].rearrange("p (b x) -> p b x", b=4)
+            hdst = raw[("h", i)][:].rearrange("p (b x) -> p b x", b=4)
             wsrc = W1[i].rearrange("(x p e) f -> p x (e f)", x=4, e=2)
-            wdst = w1_raw[i][:].rearrange("p (x y) -> p x y", x=4)
+            wdst = raw[("w1", i)][:].rearrange("p (x y) -> p x y", x=4)
             if i == 0:
                 nc.sync.dma_start(out=hdst[:, 0:2, :], in_=hsrc[:, 0:2, :])
                 nc.sync.dma_start(out=wdst[:, 0:2, :], in_=wsrc[:, 0:2, :])
@@ -54,111 +66,100 @@ def tile_multiheadgeneralizedpooling_pa_kernel(tc, h_heads, attention_mask, W1, 
             else:
                 nc.sync.dma_start(out=hdst, in_=hsrc)
                 nc.sync.dma_start(out=wdst, in_=wsrc)
-            nc.sync.dma_start(out=w2_raw[i][:], in_=W2[i].rearrange("(p e) k -> p (e k)", e=2))
-        nc.scalar.dma_start(out=b1_raw[0:16, :], in_=b1.rearrange("i (r k) -> (i r) k", k=256))
-        nc.gpsimd.dma_start(
-            out=mask_raw[:], in_=attention_mask.rearrange("b s -> (b s)").partition_broadcast(P)
-        )
-
-        tpb = psum.tile([P, 4, P], F32, tag="tp", name="tpb")
-        nc.tensor.transpose(out=tpb[:, 0, :], in_=b1_raw[:].bitcast(F32), identity=ident[:])
-        bias_w = keep.tile([P, 16], F32, name="bias_w")
-        nc.vector.tensor_copy(out=bias_w[:], in_=tpb[:, 0, 0:16])
-        bias = keep.tile([P, 32], F32, name="bias")
-        nc.vector.tensor_copy(out=bias[:], in_=bias_w[:].bitcast(BF16))
-
-        nlnm = keep.tile([P, 1024], F32, name="nlnm")
-        nc.scalar.activation(
-            out=nlnm[:].rearrange("q (b n p) -> q b n p", b=4, n=2),
-            in_=mask_raw[:].rearrange("q (b p n) -> q b n p", b=4, n=2),
-            func=ACT.Ln,
-        )
-        nc.vector.tensor_scalar_mul(out=nlnm[:], in0=nlnm[:], scalar1=-1.0)
-
-        num = keep.tile([P, 32], F32, name="num")
-        den = keep.tile([P, 32], F32, name="den")
-
-        hT_b = [None] * NH
-        w1T_b = [None] * NH
-        w2c = [None] * NH
-        w2s = [None] * NH
-
-        def prep(i):
-            hw = h_raw[i][:].bitcast(F32)
-            ww = w1_raw[i][:].bitcast(F32)
-            vw = w2_raw[i][:].bitcast(F32)
-            hT = keep.tile([P, 1024], F32, name="hT%d" % i)
-            w1T = keep.tile([P, 1024], F32, name="w1T%d" % i)
-            w2g = keep.tile([P, 1024], F32, name="w2g%d" % i, align_bytes=64)
-            for half in range(2):
-                tp = psum.tile([P, 4, P], F32, tag="tp", name="tph")
-                for k in range(4):
-                    blk = half * 4 + k
-                    nc.tensor.transpose(out=tp[:, k, :], in_=hw[:, blk * P:(blk + 1) * P], identity=ident[:])
-                nc.vector.tensor_copy(
-                    out=hT[:, half * 512:(half + 1) * 512], in_=tp[:].rearrange("q k p -> q (k p)")
+            nc.sync.dma_start(out=raw[("w2", i)][:], in_=W2[i].rearrange("(p e) k -> p (e k)", e=2))
+            if i == 0:
+                nc.sync.dma_start(
+                    out=mask_raw[:], in_=attention_mask.rearrange("b s -> (b s)").partition_broadcast(P)
                 )
-                tp = psum.tile([P, 4, P], F32, tag="tp", name="tpw")
-                for k in range(4):
-                    blk = half * 4 + k
-                    nc.tensor.transpose(out=tp[:, k, :], in_=ww[:, blk * P:(blk + 1) * P], identity=ident[:])
-                nc.scalar.copy(
-                    out=w1T[:, half * 512:(half + 1) * 512], in_=tp[:].rearrange("q k p -> q (k p)")
-                )
-            for g in range(2):
-                tp = psum.tile([P, 4, P], F32, tag="tp", name="tpv")
-                for e in range(2):
-                    for u in range(2):
-                        off = e * 512 + (g * 2 + u) * P
-                        nc.tensor.transpose(out=tp[:, e * 2 + u, :], in_=vw[:, off:off + P], identity=ident[:])
-                nc.scalar.copy(
-                    out=w2g[:, g * 512:(g + 1) * 512].rearrange("q (e p u) -> q e p u", e=2, u=2),
-                    in_=tp[:].rearrange("q (e u) p -> q e p u", e=2),
-                )
-            codes = keep.tile([P, 512], U32, name="w2c%d" % i, align_bytes=64)
-            scales = keep.tile([P, 512], U8, name="w2s%d" % i, align_bytes=64)
-            nc.vector.quantize_mx(out=codes[:].bitcast(FP8X4), scales=scales[:], in_=w2g[:].bitcast(BF16))
-            hT_b[i] = hT[:].bitcast(BF16).rearrange("q (m e) -> q m e", e=2)
-            w1T_b[i] = w1T[:].bitcast(BF16).rearrange("q (m e) -> q m e", e=2)
-            w2c[i] = codes
-            w2s[i] = scales
 
-        def first_matmul(i, c, g, hc, hs):
-            hidp = work.tile([P, 4, 512], BF16, tag="hidp", name="hidp")
+        def turn(kind, i, half):
+            words = raw[(kind, i)][:].bitcast(F32)
+            bank = psum.tile([P, 4, P], F32, tag="aux", name="bank_" + kind, bufs=4)
+            for k in range(4):
+                if kind == "w2":
+                    off = (k // 2) * 512 + (half * 2 + k % 2) * P
+                else:
+                    off = (half * 4 + k) * P
+                nc.tensor.transpose(out=bank[:, k, :], in_=words[:, off:off + P], identity=ident[:])
+            return bank
+
+        def copy_out(kind, i, half, bank, on_vector):
+            dst = turned[(kind, i)][:, half * 512:(half + 1) * 512]
+            if kind == "w2":
+                dst = dst.rearrange("q (e p u) -> q e p u", e=2, u=2)
+                src = bank[:].rearrange("q (e u) p -> q e p u", e=2)
+            else:
+                src = bank[:].rearrange("q k p -> q (k p)")
+            if on_vector:
+                nc.vector.tensor_copy(out=dst, in_=src)
+            else:
+                nc.scalar.copy(out=dst, in_=src)
+
+        def quantise_w2(i):
+            nc.vector.quantize_mx(
+                out=w2c[i][:].bitcast(FP8X4), scales=w2s[i][:], in_=turned[("w2", i)][:].bitcast(BF16)
+            )
+
+        pre = {}
+        hidp = {}
+        grouped = {}
+        codes = {}
+        att = {}
+        tneg = {}
+        minv = {}
+        ex = {}
+
+        def first_matmul(q):
+            i, c, g = q // 4, (q // 2) % 2, q % 2
             for t in range(4):
                 blk = g * 4 + t
-                pre = psum.tile([P, 512], F32, tag="pre", name="pre", bufs=4)
+                pre[(q, t)] = psum.tile([P, 512], F32, tag="pre", name="pre", bufs=4)
                 for e in range(2):
                     nc.tensor.matmul(
-                        out=pre[:],
+                        out=pre[(q, t)][:],
                         lhsT=w1T_b[i][:, blk * P:(blk + 1) * P, e],
                         rhs=hT_b[i][:, c * 512:(c + 1) * 512, e],
                         start=(e == 0),
                         stop=(e == 1),
                     )
-                col = i * 8 + blk
+
+        def relu_out(q):
+            i, g = q // 4, q % 2
+            hidp[q] = work.tile([P, 4, 512], BF16, tag="hidp", name="hidp")
+            for t in range(4):
+                col = i * 8 + g * 4 + t
                 nc.scalar.activation(
-                    out=hidp[:, t, :], in_=pre[:], func=ACT.Relu, bias=bias[:, col:col + 1], scale=1.0
+                    out=hidp[q][:, t, :], in_=pre[(q, t)][:], func=ACT.Relu, bias=bias[:, col:col + 1], scale=1.0
                 )
-            grouped = work.tile([P, 512, 4], BF16, tag="grouped", name="grouped", align_bytes=64)
+
+        def regroup(q):
+            grouped[q] = work.tile([P, 512, 4], BF16, tag="grouped", name="grouped", align_bytes=64)
             nc.vector.tensor_copy(
-                out=grouped[:].rearrange("p (a r) t -> p a t r", r=4),
-                in_=hidp[:].rearrange("p t (a r) -> p a t r", r=4),
-            )
-            nc.vector.quantize_mx(
-                out=hc[:, g, :].bitcast(FP8X4),
-                scales=hs[:, g, :],
-                in_=grouped[:].rearrange("p w t -> p (w t)"),
+                out=grouped[q][:].rearrange("p (a r) t -> p a t r", r=4),
+                in_=hidp[q][:].rearrange("p t (a r) -> p a t r", r=4),
             )
 
-        def second_matmul(i, hc, hs):
-            att = []
+        def quantise(q):
+            j, g = q // 2, q % 2
+            if g == 0:
+                codes[j] = (
+                    work.tile([P, 2, 512], U32, tag="hc", name="hc", align_bytes=64),
+                    work.tile([P, 2, 512], U8, tag="hs", name="hs", align_bytes=64),
+                )
+            hc, hs = codes[j]
+            nc.vector.quantize_mx(
+                out=hc[:, g, :].bitcast(FP8X4), scales=hs[:, g, :], in_=grouped[q][:].rearrange("p w t -> p (w t)")
+            )
+
+        def second_matmul(j):
+            i = j // 2
+            hc, hs = codes[j]
             for e in range(2):
-                a = psum.tile([P, 512], F32, tag="att", name="att")
+                att[(j, e)] = psum.tile([P, 512], F32, tag="aux", name="att", bufs=4)
                 for g in range(2):
                     lo = (g * 2 + e) * P
                     nc.tensor.matmul_mx(
-                        out=a[:],
+                        out=att[(j, e)][:],
                         lhsT=w2c[i][:, lo:lo + P].bitcast(FP8X4),
                         lhsT_scale=w2s[i][:, lo:lo + P],
                         rhs=hc[:, g, :].bitcast(FP8X4),
@@ -166,55 +167,138 @@ def tile_multiheadgeneralizedpooling_pa_kernel(tc, h_heads, attention_mask, W1, 
                         start=(g == 0),
                         stop=(g == 1),
                     )
-                att.append(a)
-            return att
 
-        def softmax(i, c, att):
-            tneg = work.tile([P, 2, 512], F32, tag="tneg", name="tneg")
-            for e in range(2):
-                nc.vector.tensor_tensor(
-                    out=tneg[:, e, :], in0=nlnm[:, c * 512:(c + 1) * 512], in1=att[e][:], op=ALU.subtract
-                )
-            minv = work.tile([P, 4], F32, tag="minv", name="minv")
-            nc.vector.tensor_reduce(
-                out=minv[:], in_=tneg[:].rearrange("p e (s w) -> p (e s) w", w=256), axis=AX.X, op=ALU.min
-            )
-            for e in range(2):
-                for s in range(2):
-                    col = e * 16 + (2 * c + s) * 4 + i
-                    ex = work.tile([P, 256], F32, tag="ex", name="ex", bufs=4)
-                    nc.scalar.activation(
-                        out=ex[:],
-                        in_=tneg[:, e, s * 256:(s + 1) * 256],
-                        func=ACT.Exp,
-                        bias=minv[:, e * 2 + s:e * 2 + s + 1],
-                        scale=-1.0,
-                        accum_out=den[:, col:col + 1],
-                    )
-                    junk = work.tile([P, 256], F32, tag="junk", name="junk", bufs=2)
-                    lo = c * 512 + s * 256
-                    nc.vector.scalar_tensor_tensor(
-                        out=junk[:],
-                        in0=ex[:],
-                        scalar=1.0,
-                        in1=hT_b[i][:, lo:lo + 256, e],
-                        op0=ALU.mult,
-                        op1=ALU.mult,
-                        accum_out=num[:, col:col + 1],
-                    )
-
-        prep(0)
-        for j in range(2 * NH):
-            i = j // 2
+        def add_mask(j, e):
             c = j % 2
-            hc = work.tile([P, 2, 512], U32, tag="hc", name="hc", align_bytes=64)
-            hs = work.tile([P, 2, 512], U8, tag="hs", name="hs", align_bytes=64)
-            first_matmul(i, c, 0, hc, hs)
-            first_matmul(i, c, 1, hc, hs)
-            if c == 0 and i + 1 < NH:
-                prep(i + 1)
-            att = second_matmul(i, hc, hs)
-            softmax(i, c, att)
+            if e == 0:
+                tneg[j] = work.tile([P, 2, 512], F32, tag="tneg", name="tneg")
+                minv[j] = work.tile([P, 4], F32, tag="minv", name="minv")
+            nc.vector.tensor_tensor(
+                out=tneg[j][:, e, :], in0=nlnm[:, c * 512:(c + 1) * 512], in1=att[(j, e)][:], op=ALU.subtract
+            )
+
+        def find_min(j, e):
+            nc.vector.tensor_reduce(
+                out=minv[j][:, 2 * e:2 * e + 2],
+                in_=tneg[j][:, e, :].rearrange("p (s w) -> p s w", w=256),
+                axis=AX.X,
+                op=ALU.min,
+            )
+
+        def column(j, k):
+            i, c, e, s = j // 2, j % 2, k // 2, k % 2
+            return e * 16 + (2 * c + s) * 4 + i
+
+        def exponent(j, k):
+            e, s = k // 2, k % 2
+            col = column(j, k)
+            ex[(j, k)] = work.tile([P, 256], F32, tag="ex", name="ex", bufs=8)
+            nc.scalar.activation(
+                out=ex[(j, k)][:],
+                in_=tneg[j][:, e, s * 256:(s + 1) * 256],
+                func=ACT.Exp,
+                bias=minv[j][:, k:k + 1],
+                scale=-1.0,
+                accum_out=den[:, col:col + 1],
+            )
+
+        def weighted_sum(j, k):
+            i, c, e, s = j // 2, j % 2, k // 2, k % 2
+            col = column(j, k)
+            lo = c * 512 + s * 256
+            junk = work.tile([P, 256], F32, tag="junk", name="junk", bufs=2)
+            nc.vector.scalar_tensor_tensor(
+                out=junk[:],
+                in0=ex[(j, k)][:],
+                scalar=1.0,
+                in1=hT_b[i][:, lo:lo + 256, e],
+                op0=ALU.mult,
+                op1=ALU.mult,
+                accum_out=num[:, col:col + 1],
+            )
+
+        bank = turn("h", 0, 0)
+        copy_out("h", 0, 0, bank, True)
+        bank = turn("w1", 0, 0)
+        copy_out("w1", 0, 0, bank, False)
+        bank_b = psum.tile([P, 4, P], F32, tag="aux", name="bank_b", bufs=4)
+        nc.tensor.transpose(out=bank_b[:, 0, :], in_=b1_raw[:].bitcast(F32), identity=ident[:])
+        nc.vector.tensor_copy(out=bias_w[:], in_=bank_b[:, 0, 0:16])
+        nc.vector.tensor_copy(out=bias[:], in_=bias_w[:].bitcast(BF16))
+        bank = turn("w1", 0, 1)
+        copy_out("w1", 0, 1, bank, False)
+        bank = turn("h", 0, 1)
+        copy_out("h", 0, 1, bank, True)
+        first_matmul(0)
+
+        for j in range(CHUNKS + 2):
+            body = j < CHUNKS
+            soft = 1 <= j <= CHUNKS
+            sums = 2 <= j
+            nxt = j // 2 + 1
+            prep = body and nxt < NH
+            if j % 2 == 0:
+                todo = (("h", 0), ("h", 1), ("w1", 0))
+            else:
+                todo = (("w1", 1), ("w2", 0), ("w2", 1))
+            if soft:
+                second_matmul(j - 1)
+            if body and j >= 2 and j % 2 == 0:
+                quantise_w2(j // 2)
+            if sums:
+                for k in range(3):
+                    weighted_sum(j - 2, k)
+            if soft:
+                add_mask(j - 1, 0)
+                if not body:
+                    find_min(j - 1, 0)
+                add_mask(j - 1, 1)
+                if not body:
+                    find_min(j - 1, 1)
+            if body:
+                relu_out(2 * j)
+                first_matmul(2 * j + 1)
+                if j == 0:
+                    bank_v = [turn("w2", 0, 0), turn("w2", 0, 1)]
+                if prep:
+                    banks = [turn(kind, nxt, half) for kind, half in todo[0:2]]
+                regroup(2 * j)
+                if j == 0:
+                    copy_out("w2", 0, 0, bank_v[0], True)
+                if prep:
+                    banks.append(turn(todo[2][0], nxt, todo[2][1]))
+                if soft:
+                    find_min(j - 1, 0)
+                quantise(2 * j)
+                if j == 0:
+                    copy_out("w2", 0, 1, bank_v[1], True)
+                if soft:
+                    find_min(j - 1, 1)
+                relu_out(2 * j + 1)
+                if 2 * j + 2 < HALVES:
+                    first_matmul(2 * j + 2)
+                regroup(2 * j + 1)
+                if j == 0:
+                    quantise_w2(0)
+            if sums:
+                weighted_sum(j - 2, 3)
+            if body:
+                quantise(2 * j + 1)
+            if j == 0:
+                nc.scalar.activation(
+                    out=nlnm[:].rearrange("q (b n p) -> q b n p", b=4, n=2),
+                    in_=mask_raw[:].rearrange("q (b p n) -> q b n p", b=4, n=2),
+                    func=ACT.Ln,
+                )
+                nc.gpsimd.tensor_scalar(
+                    out=nlnm[:], in0=nlnm[:], scalar1=-1.0, scalar2=0.0, op0=ALU.mult, op1=ALU.add
+                )
+            if prep:
+                for (kind, half), bank in zip(todo, banks):
+                    copy_out(kind, nxt, half, bank, False)
+            if soft:
+                for k in range(4):
+                    exponent(j - 1, k)
 
         rden = keep.tile([P, 32], F32, name="rden")
         nc.vector.reciprocal(out=rden[:], in_=den[:])
@@ -224,12 +308,12 @@ def tile_multiheadgeneralizedpooling_pa_kernel(tc, h_heads, attention_mask, W1, 
             in1=rden[:].rearrange("p (e x) -> p e x", e=2),
             op=ALU.mult,
         )
-        tpo = psum.tile([P, 4, P], F32, tag="tp", name="tpo")
+        bank_o = psum.tile([P, 4, P], F32, tag="aux", name="bank_o", bufs=4)
         for e in range(2):
-            nc.tensor.transpose(out=tpo[:, e, :], in_=res[:, e, :], identity=ident[:])
+            nc.tensor.transpose(out=bank_o[:, e, :], in_=res[:, e, :], identity=ident[:])
         o_sb = keep.tile([P, 256], F32, name="o_sb")
         nc.scalar.copy(
             out=o_sb[0:16, :].rearrange("r (p e) -> r p e", e=2),
-            in_=tpo[0:16, 0:2, :].rearrange("r e p -> r p e"),
+            in_=bank_o[0:16, 0:2, :].rearrange("r e p -> r p e"),
         )
         nc.sync.dma_start(out=out.rearrange("b (i f) -> (b i) f", i=4), in_=o_sb[0:16, :])

@@ -39,7 +39,9 @@ def tile_multiheadgeneralizedpooling_pa_kernel(tc, h_heads, attention_mask, W1, 
         hT_b = [turned[("h", i)][:].bitcast(BF16).rearrange("q (m e) -> q m e", e=2) for i in range(NH)]
         w1T_b = [turned[("w1", i)][:].bitcast(BF16).rearrange("q (m e) -> q m e", e=2) for i in range(NH)]
         b1_raw = keep.tile([P, 256], BF16, name="b1_raw")
-        mask_raw = keep.tile([P, 1024], BF16, name="mask_raw")
+        mask_row = keep.tile([P, 1024], BF16, name="mask_row")
+        ones = keep.tile([P, P], BF16, name="ones")
+        warm = keep.tile([P, 1], F32, name="warm")
         res = keep.tile([P, 2, P], F32, name="res")
         ident = keep.tile([P, P], F32, name="ident")
         bias_w = keep.tile([P, 16], F32, name="bias_w")
@@ -48,11 +50,12 @@ def tile_multiheadgeneralizedpooling_pa_kernel(tc, h_heads, attention_mask, W1, 
         num = keep.tile([P, 32], F32, name="num")
         den = keep.tile([P, 32], F32, name="den")
 
+        nc.vector.memset(mask_row[:], 0.0)
+        nc.vector.memset(ones[:], 1.0)
         nc.vector.memset(b1_raw[:], 0.0)
         nc.vector.memset(res[:], 0.0)
         make_identity(nc, ident[:])
 
-        nc.scalar.dma_start(out=b1_raw[0:16, :], in_=b1.rearrange("i (r k) -> (i r) k", k=256))
         for i in range(NH):
             hsrc = h_heads[i].rearrange("b (p n) f -> p b (n f)", n=2)
             hdst = raw[("h", i)][:].rearrange("p (b x) -> p b x", b=4)
@@ -60,6 +63,8 @@ def tile_multiheadgeneralizedpooling_pa_kernel(tc, h_heads, attention_mask, W1, 
             wdst = raw[("w1", i)][:].rearrange("p (x y) -> p x y", x=4)
             if i == 0:
                 nc.sync.dma_start(out=hdst[:, 0:2, :], in_=hsrc[:, 0:2, :])
+                nc.sync.dma_start(out=mask_row[0:1, :], in_=attention_mask.rearrange("(o b) s -> o (b s)", o=1))
+                nc.sync.dma_start(out=b1_raw[0:16, :], in_=b1.rearrange("i (r k) -> (i r) k", k=256))
                 nc.sync.dma_start(out=wdst[:, 0:2, :], in_=wsrc[:, 0:2, :])
                 nc.sync.dma_start(out=wdst[:, 2:4, :], in_=wsrc[:, 2:4, :])
                 nc.sync.dma_start(out=hdst[:, 2:4, :], in_=hsrc[:, 2:4, :])
@@ -67,10 +72,6 @@ def tile_multiheadgeneralizedpooling_pa_kernel(tc, h_heads, attention_mask, W1, 
                 nc.sync.dma_start(out=hdst, in_=hsrc)
                 nc.sync.dma_start(out=wdst, in_=wsrc)
             nc.sync.dma_start(out=raw[("w2", i)][:], in_=W2[i].rearrange("(p e) k -> p (e k)", e=2))
-            if i == 0:
-                nc.sync.dma_start(
-                    out=mask_raw[:], in_=attention_mask.rearrange("b s -> (b s)").partition_broadcast(P)
-                )
 
         def turn(kind, i, half):
             words = raw[(kind, i)][:].bitcast(F32)
@@ -156,7 +157,8 @@ def tile_multiheadgeneralizedpooling_pa_kernel(tc, h_heads, attention_mask, W1, 
             hc, hs = codes[j]
             for e in range(2):
                 att[(j, e)] = psum.tile([P, 512], F32, tag="aux", name="att", bufs=4)
-                for g in range(2):
+            for g in range(2):
+                for e in range(2):
                     lo = (g * 2 + e) * P
                     nc.tensor.matmul_mx(
                         out=att[(j, e)][:],
@@ -217,16 +219,28 @@ def tile_multiheadgeneralizedpooling_pa_kernel(tc, h_heads, attention_mask, W1, 
                 accum_out=num[:, col:col + 1],
             )
 
+        nc.scalar.activation(out=warm[:], in_=ones[:, 0:1], func=ACT.Ln)
         bank = turn("h", 0, 0)
         copy_out("h", 0, 0, bank, True)
         bank = turn("w1", 0, 0)
-        copy_out("w1", 0, 0, bank, False)
+        copy_out("w1", 0, 0, bank, True)
+        for half in range(2):
+            spread = psum.tile([P, 512], F32, tag="pre", name="spread", bufs=4)
+            nc.tensor.matmul(
+                out=spread[:], lhsT=ones[:], rhs=mask_row[:, half * 512:(half + 1) * 512], start=True, stop=True
+            )
+            nc.scalar.activation(
+                out=nlnm[:, half * 512:(half + 1) * 512].rearrange("q (b n p) -> q b n p", b=2, n=2),
+                in_=spread[:].rearrange("q (b p n) -> q b n p", b=2, n=2),
+                func=ACT.Ln,
+            )
+        nc.gpsimd.tensor_scalar(out=nlnm[:], in0=nlnm[:], scalar1=-1.0, scalar2=0.0, op0=ALU.mult, op1=ALU.add)
         bank_b = psum.tile([P, 4, P], F32, tag="aux", name="bank_b", bufs=4)
         nc.tensor.transpose(out=bank_b[:, 0, :], in_=b1_raw[:].bitcast(F32), identity=ident[:])
         nc.vector.tensor_copy(out=bias_w[:], in_=bank_b[:, 0, 0:16])
         nc.vector.tensor_copy(out=bias[:], in_=bias_w[:].bitcast(BF16))
         bank = turn("w1", 0, 1)
-        copy_out("w1", 0, 1, bank, False)
+        copy_out("w1", 0, 1, bank, True)
         bank = turn("h", 0, 1)
         copy_out("h", 0, 1, bank, True)
         first_matmul(0)
@@ -285,17 +299,10 @@ def tile_multiheadgeneralizedpooling_pa_kernel(tc, h_heads, attention_mask, W1, 
             if body:
                 quantise(2 * j + 1)
             if j == 0:
-                nc.scalar.activation(
-                    out=nlnm[:].rearrange("q (b n p) -> q b n p", b=4, n=2),
-                    in_=mask_raw[:].rearrange("q (b p n) -> q b n p", b=4, n=2),
-                    func=ACT.Ln,
-                )
-                nc.gpsimd.tensor_scalar(
-                    out=nlnm[:], in0=nlnm[:], scalar1=-1.0, scalar2=0.0, op0=ALU.mult, op1=ALU.add
-                )
+                nc.scalar.activation(out=warm[:], in_=res[:, 0, 0:1], func=ACT.Exp)
             if prep:
                 for (kind, half), bank in zip(todo, banks):
-                    copy_out(kind, nxt, half, bank, False)
+                    copy_out(kind, nxt, half, bank, j == 0 and kind == "h")
             if soft:
                 for k in range(4):
                     exponent(j - 1, k)

@@ -252,9 +252,9 @@ def tile_multiheadgeneralizedpooling_pa_kernel(tc, h_heads, attention_mask, W1, 
             nxt = j // 2 + 1
             prep = body and nxt < NH
             if j % 2 == 0:
-                todo = (("h", 0), ("h", 1), ("w1", 0))
+                todo = (("w1", 0), ("h", 0), ("h", 1))
             else:
-                todo = (("w1", 1), ("w2", 0), ("w2", 1))
+                todo = (("w2", 0), ("w2", 1), ("w1", 1))
             if soft:
                 second_matmul(j - 1)
             if body and j >= 2 and j % 2 == 0:
@@ -264,36 +264,29 @@ def tile_multiheadgeneralizedpooling_pa_kernel(tc, h_heads, attention_mask, W1, 
                     weighted_sum(j - 2, k)
             if soft:
                 add_mask(j - 1, 0)
-                if not body:
-                    find_min(j - 1, 0)
                 add_mask(j - 1, 1)
-                if not body:
-                    find_min(j - 1, 1)
+                find_min(j - 1, 0)
             if body:
                 relu_out(2 * j)
-                first_matmul(2 * j + 1)
                 if j == 0:
                     bank_v = [turn("w2", 0, 0), turn("w2", 0, 1)]
-                if prep:
-                    banks = [turn(kind, nxt, half) for kind, half in todo[0:2]]
-                regroup(2 * j)
+                first_matmul(2 * j + 1)
                 if j == 0:
                     copy_out("w2", 0, 0, bank_v[0], True)
-                if prep:
-                    banks.append(turn(todo[2][0], nxt, todo[2][1]))
-                if soft:
-                    find_min(j - 1, 0)
-                quantise(2 * j)
-                if j == 0:
                     copy_out("w2", 0, 1, bank_v[1], True)
-                if soft:
-                    find_min(j - 1, 1)
+                if prep:
+                    banks = [turn(kind, nxt, half) for kind, half in todo]
+                regroup(2 * j)
+                if j == 0:
+                    quantise_w2(0)
+            if soft:
+                find_min(j - 1, 1)
+            if body:
+                quantise(2 * j)
                 relu_out(2 * j + 1)
                 if 2 * j + 2 < HALVES:
                     first_matmul(2 * j + 2)
                 regroup(2 * j + 1)
-                if j == 0:
-                    quantise_w2(0)
             if sums:
                 weighted_sum(j - 2, 3)
             if body:

from contextlib import ExitStack

import concourse.mybir as mybir
from concourse.masks import make_identity

FLOPS = 2 * 2 * 4 * 1024 * 1024 * 256

F32 = mybir.dt.float32
BF16 = mybir.dt.bfloat16
U32 = mybir.dt.uint32
U8 = mybir.dt.uint8
FP8X4 = mybir.dt.float8_e4m3fn_x4
ACT = mybir.ActivationFunctionType
ALU = mybir.AluOpType
AX = mybir.AxisListType

P = 128
NH = 4
CHUNKS = 2 * NH
HALVES = 2 * CHUNKS


def tile_multiheadgeneralizedpooling_pa_kernel(tc, h_heads, attention_mask, W1, b1, W2, out):
    nc = tc.nc
    with ExitStack() as ctx:
        keep = ctx.enter_context(tc.tile_pool(name="keep", bufs=1))
        work = ctx.enter_context(tc.tile_pool(name="work", bufs=3))
        psum = ctx.enter_context(tc.psum_pool(name="psum", bufs=2))
        ctx.enter_context(tc.manual_schedule())

        raw = {}
        turned = {}
        for i in range(NH):
            for kind in ("h", "w1", "w2"):
                raw[(kind, i)] = keep.tile([P, 2048], BF16, name="raw_%s%d" % (kind, i))
                turned[(kind, i)] = keep.tile([P, 1024], F32, name="turned_%s%d" % (kind, i), align_bytes=64)
        w2c = [keep.tile([P, 512], U32, name="w2c%d" % i, align_bytes=64) for i in range(NH)]
        w2s = [keep.tile([P, 512], U8, name="w2s%d" % i, align_bytes=64) for i in range(NH)]
        hT_b = [turned[("h", i)][:].bitcast(BF16).rearrange("q (m e) -> q m e", e=2) for i in range(NH)]
        w1T_b = [turned[("w1", i)][:].bitcast(BF16).rearrange("q (m e) -> q m e", e=2) for i in range(NH)]
        b1_raw = keep.tile([P, 256], BF16, name="b1_raw")
        mask_row = keep.tile([P, 1024], BF16, name="mask_row")
        ones = keep.tile([P, P], BF16, name="ones")
        warm = keep.tile([P, 1], F32, name="warm")
        res = keep.tile([P, 2, P], F32, name="res")
        ident = keep.tile([P, P], F32, name="ident")
        bias_w = keep.tile([P, 16], F32, name="bias_w")
        bias = keep.tile([P, 32], F32, name="bias")
        nlnm = keep.tile([P, 1024], F32, name="nlnm")
        num = keep.tile([P, 32], F32, name="num")
        den = keep.tile([P, 32], F32, name="den")

        nc.vector.memset(mask_row[:], 0.0)
        nc.vector.memset(ones[:], 1.0)
        nc.vector.memset(b1_raw[:], 0.0)
        nc.vector.memset(res[:], 0.0)
        make_identity(nc, ident[:])

        for i in range(NH):
            hsrc = h_heads[i].rearrange("b (p n) f -> p b (n f)", n=2)
            hdst = raw[("h", i)][:].rearrange("p (b x) -> p b x", b=4)
            wsrc = W1[i].rearrange("(x p e) f -> p x (e f)", x=4, e=2)
            wdst = raw[("w1", i)][:].rearrange("p (x y) -> p x y", x=4)
            if i == 0:
                nc.sync.dma_start(out=hdst[:, 0:2, :], in_=hsrc[:, 0:2, :])
                nc.sync.dma_start(out=mask_row[0:1, :], in_=attention_mask.rearrange("(o b) s -> o (b s)", o=1))
                nc.sync.dma_start(out=b1_raw[0:16, :], in_=b1.rearrange("i (r k) -> (i r) k", k=256))
                nc.sync.dma_start(out=wdst[:, 0:2, :], in_=wsrc[:, 0:2, :])
                nc.sync.dma_start(out=wdst[:, 2:4, :], in_=wsrc[:, 2:4, :])
                nc.sync.dma_start(out=hdst[:, 2:4, :], in_=hsrc[:, 2:4, :])
            else:
                nc.sync.dma_start(out=hdst, in_=hsrc)
                nc.sync.dma_start(out=wdst, in_=wsrc)
            nc.sync.dma_start(out=raw[("w2", i)][:], in_=W2[i].rearrange("(p e) k -> p (e k)", e=2))

        def turn(kind, i, half):
            words = raw[(kind, i)][:].bitcast(F32)
            bank = psum.tile([P, 4, P], F32, tag="aux", name="bank_" + kind, bufs=4)
            for k in range(4):
                if kind == "w2":
                    off = (k // 2) * 512 + (half * 2 + k % 2) * P
                else:
                    off = (half * 4 + k) * P
                nc.tensor.transpose(out=bank[:, k, :], in_=words[:, off:off + P], identity=ident[:])
            return bank

        def copy_out(kind, i, half, bank, on_vector):
            dst = turned[(kind, i)][:, half * 512:(half + 1) * 512]
            if kind == "w2":
                dst = dst.rearrange("q (e p u) -> q e p u", e=2, u=2)
                src = bank[:].rearrange("q (e u) p -> q e p u", e=2)
            else:
                src = bank[:].rearrange("q k p -> q (k p)")
            if on_vector:
                nc.vector.tensor_copy(out=dst, in_=src)
            else:
                nc.scalar.copy(out=dst, in_=src)

        def quantise_w2(i):
            nc.vector.quantize_mx(
                out=w2c[i][:].bitcast(FP8X4), scales=w2s[i][:], in_=turned[("w2", i)][:].bitcast(BF16)
            )

        pre = {}
        hidp = {}
        grouped = {}
        codes = {}
        att = {}
        tneg = {}
        minv = {}
        ex = {}

        def first_matmul(q):
            i, c, g = q // 4, (q // 2) % 2, q % 2
            for t in range(4):
                blk = g * 4 + t
                pre[(q, t)] = psum.tile([P, 512], F32, tag="pre", name="pre", bufs=4)
                for e in range(2):
                    nc.tensor.matmul(
                        out=pre[(q, t)][:],
                        lhsT=w1T_b[i][:, blk * P:(blk + 1) * P, e],
                        rhs=hT_b[i][:, c * 512:(c + 1) * 512, e],
                        start=(e == 0),
                        stop=(e == 1),
                    )

        def relu_out(q):
            i, g = q // 4, q % 2
            hidp[q] = work.tile([P, 4, 512], BF16, tag="hidp", name="hidp")
            for t in range(4):
                col = i * 8 + g * 4 + t
                nc.scalar.activation(
                    out=hidp[q][:, t, :], in_=pre[(q, t)][:], func=ACT.Relu, bias=bias[:, col:col + 1], scale=1.0
                )

        def regroup(q):
            grouped[q] = work.tile([P, 512, 4], BF16, tag="grouped", name="grouped", align_bytes=64)
            nc.vector.tensor_copy(
                out=grouped[q][:].rearrange("p (a r) t -> p a t r", r=4),
                in_=hidp[q][:].rearrange("p t (a r) -> p a t r", r=4),
            )

        def quantise(q):
            j, g = q // 2, q % 2
            if g == 0:
                codes[j] = (
                    work.tile([P, 2, 512], U32, tag="hc", name="hc", align_bytes=64),
                    work.tile([P, 2, 512], U8, tag="hs", name="hs", align_bytes=64),
                )
            hc, hs = codes[j]
            nc.vector.quantize_mx(
                out=hc[:, g, :].bitcast(FP8X4), scales=hs[:, g, :], in_=grouped[q][:].rearrange("p w t -> p (w t)")
            )

        def second_matmul(j):
            i = j // 2
            hc, hs = codes[j]
            for e in range(2):
                att[(j, e)] = psum.tile([P, 512], F32, tag="aux", name="att", bufs=4)
            for g in range(2):
                for e in range(2):
                    lo = (g * 2 + e) * P
                    nc.tensor.matmul_mx(
                        out=att[(j, e)][:],
                        lhsT=w2c[i][:, lo:lo + P].bitcast(FP8X4),
                        lhsT_scale=w2s[i][:, lo:lo + P],
                        rhs=hc[:, g, :].bitcast(FP8X4),
                        rhs_scale=hs[:, g, :],
                        start=(g == 0),
                        stop=(g == 1),
                    )

        def add_mask(j, e):
            c = j % 2
            if e == 0:
                tneg[j] = work.tile([P, 2, 512], F32, tag="tneg", name="tneg")
                minv[j] = work.tile([P, 4], F32, tag="minv", name="minv")
            nc.vector.tensor_tensor(
                out=tneg[j][:, e, :], in0=nlnm[:, c * 512:(c + 1) * 512], in1=att[(j, e)][:], op=ALU.subtract
            )

        def find_min(j, e):
            nc.vector.tensor_reduce(
                out=minv[j][:, 2 * e:2 * e + 2],
                in_=tneg[j][:, e, :].rearrange("p (s w) -> p s w", w=256),
                axis=AX.X,
                op=ALU.min,
            )

        def column(j, k):
            i, c, e, s = j // 2, j % 2, k // 2, k % 2
            return e * 16 + (2 * c + s) * 4 + i

        def exponent(j, k):
            e, s = k // 2, k % 2
            col = column(j, k)
            ex[(j, k)] = work.tile([P, 256], F32, tag="ex", name="ex", bufs=8)
            nc.scalar.activation(
                out=ex[(j, k)][:],
                in_=tneg[j][:, e, s * 256:(s + 1) * 256],
                func=ACT.Exp,
                bias=minv[j][:, k:k + 1],
                scale=-1.0,
                accum_out=den[:, col:col + 1],
            )

        def weighted_sum(j, k):
            i, c, e, s = j // 2, j % 2, k // 2, k % 2
            col = column(j, k)
            lo = c * 512 + s * 256
            junk = work.tile([P, 256], F32, tag="junk", name="junk", bufs=2)
            nc.vector.scalar_tensor_tensor(
                out=junk[:],
                in0=ex[(j, k)][:],
                scalar=1.0,
                in1=hT_b[i][:, lo:lo + 256, e],
                op0=ALU.mult,
                op1=ALU.mult,
                accum_out=num[:, col:col + 1],
            )

        nc.scalar.activation(out=warm[:], in_=ones[:, 0:1], func=ACT.Ln)
        bank = turn("h", 0, 0)
        copy_out("h", 0, 0, bank, True)
        bank = turn("w1", 0, 0)
        copy_out("w1", 0, 0, bank, True)
        for half in range(2):
            spread = psum.tile([P, 512], F32, tag="pre", name="spread", bufs=4)
            nc.tensor.matmul(
                out=spread[:], lhsT=ones[:], rhs=mask_row[:, half * 512:(half + 1) * 512], start=True, stop=True
            )
            nc.scalar.activation(
                out=nlnm[:, half * 512:(half + 1) * 512].rearrange("q (b n p) -> q b n p", b=2, n=2),
                in_=spread[:].rearrange("q (b p n) -> q b n p", b=2, n=2),
                func=ACT.Ln,
            )
        nc.gpsimd.tensor_scalar(out=nlnm[:], in0=nlnm[:], scalar1=-1.0, scalar2=0.0, op0=ALU.mult, op1=ALU.add)
        bank_b = psum.tile([P, 4, P], F32, tag="aux", name="bank_b", bufs=4)
        nc.tensor.transpose(out=bank_b[:, 0, :], in_=b1_raw[:].bitcast(F32), identity=ident[:])
        nc.vector.tensor_copy(out=bias_w[:], in_=bank_b[:, 0, 0:16])
        nc.vector.tensor_copy(out=bias[:], in_=bias_w[:].bitcast(BF16))
        bank = turn("w1", 0, 1)
        copy_out("w1", 0, 1, bank, True)
        bank = turn("h", 0, 1)
        copy_out("h", 0, 1, bank, True)
        first_matmul(0)

        for j in range(CHUNKS + 2):
            body = j < CHUNKS
            soft = 1 <= j <= CHUNKS
            sums = 2 <= j
            nxt = j // 2 + 1
            prep = body and nxt < NH
            if j % 2 == 0:
                todo = (("w1", 0), ("h", 0), ("h", 1))
            else:
                todo = (("w2", 0), ("w2", 1), ("w1", 1))
            if soft:
                second_matmul(j - 1)
            if body and j >= 2 and j % 2 == 0:
                quantise_w2(j // 2)
            if sums:
                for k in range(3):
                    weighted_sum(j - 2, k)
            if soft:
                add_mask(j - 1, 0)
                add_mask(j - 1, 1)
                find_min(j - 1, 0)
            if body:
                relu_out(2 * j)
                if j == 0:
                    bank_v = [turn("w2", 0, 0), turn("w2", 0, 1)]
                first_matmul(2 * j + 1)
                if j == 0:
                    copy_out("w2", 0, 0, bank_v[0], True)
                    copy_out("w2", 0, 1, bank_v[1], True)
                if prep:
                    banks = [turn(kind, nxt, half) for kind, half in todo]
                regroup(2 * j)
                if j == 0:
                    quantise_w2(0)
            if soft:
                find_min(j - 1, 1)
            if body:
                quantise(2 * j)
                relu_out(2 * j + 1)
                if 2 * j + 2 < HALVES:
                    first_matmul(2 * j + 2)
                regroup(2 * j + 1)
            if sums:
                weighted_sum(j - 2, 3)
            if body:
                quantise(2 * j + 1)
            if j == 0:
                nc.scalar.activation(out=warm[:], in_=res[:, 0, 0:1], func=ACT.Exp)
            if prep:
                for (kind, half), bank in zip(todo, banks):
                    copy_out(kind, nxt, half, bank, j == 0 and kind == "h")
            if soft:
                for k in range(4):
                    exponent(j - 1, k)

        rden = keep.tile([P, 32], F32, name="rden")
        nc.vector.reciprocal(out=rden[:], in_=den[:])
        nc.vector.tensor_tensor(
            out=res[:, :, 0:16],
            in0=num[:].rearrange("p (e x) -> p e x", e=2),
            in1=rden[:].rearrange("p (e x) -> p e x", e=2),
            op=ALU.mult,
        )
        bank_o = psum.tile([P, 4, P], F32, tag="aux", name="bank_o", bufs=4)
        for e in range(2):
            nc.tensor.transpose(out=bank_o[:, e, :], in_=res[:, e, :], identity=ident[:])
        o_sb = keep.tile([P, 256], F32, name="o_sb")
        nc.scalar.copy(
            out=o_sb[0:16, :].rearrange("r (p e) -> r p e", e=2),
            in_=bank_o[0:16, 0:2, :].rearrange("r e p -> r p e"),
        )
        nc.sync.dma_start(out=out.rearrange("b (i f) -> (b i) f", i=4), in_=o_sb[0:16, :])
